import numpy as np
import ml_dtypes


def mxq(x, axis, fmt="e4m3"):
    dtype, down = {"e4m3": (ml_dtypes.float8_e4m3fn, 7), "e5m2": (ml_dtypes.float8_e5m2, 14)}[fmt]
    v = np.moveaxis(np.asarray(x, np.float32).astype(ml_dtypes.bfloat16).astype(np.float64), axis, -1)
    blocks = v.reshape(v.shape[:-1] + (-1, 32))
    amax = np.abs(blocks).max(-1, keepdims=True)
    byte = np.maximum(np.where(amax > 0, np.frexp(amax)[1] - 1 + 127, 0) - down, 1)
    scale = np.exp2(byte - 127.0)
    codes = (blocks / scale).astype(np.float32).astype(dtype).astype(np.float64)
    return np.moveaxis((codes * scale).reshape(v.shape), -1, axis)


WIDE = False


def mx_kscale(k):
    if not WIDE:
        return np.ones(k)
    levels = np.array([10, -10, 5, -5, 0])
    a = np.random.permutation(np.resize(levels, k // 512 * 4)).reshape(k // 512, 4)
    idx = np.arange(k)
    return np.exp2(a[idx // 512, idx % 128 // 32])


BF16 = ml_dtypes.bfloat16


def bf(x):
    return np.asarray(x, np.float32).astype(BF16)


def f64(x):
    return np.asarray(x).astype(np.float64)


N, T, D, B0, C, P0, V1, P1, V2 = 2, 512, 1024, 2046, 2, 512, 2048, 512, 1024
MU = 0.25
SIG = 2.0


def softmax(v):
    e = np.exp(v - v.max(-1, keepdims=True))
    return e / e.sum(-1, keepdims=True)


def setup_inputs():
    s, t = mx_kscale(D), mx_kscale(P0)
    hw = np.random.standard_normal((D, B0 + C)) * SIG / np.sqrt(D)
    hw[:, B0:] = hw[:, B0:] / SIG + (np.log(B0) + 0.5 * SIG * SIG) / (MU * D)
    return {"x": bf((np.random.standard_normal((N, T, D)) + MU) * s),
            "head_weight": bf(hw / s[:, None]),
            "tail_proj_0": bf(np.random.standard_normal((D, P0)) / np.sqrt(D) / s[:, None] * t),
            "tail_w_0": bf(np.random.standard_normal((P0, V1)) * SIG / np.sqrt(P0) / t[:, None])}


def reference(x, head_weight, tail_proj_0, tail_w_0):
    xq = mxq(f64(x), 2, "e4m3")
    head_sm = softmax(xq @ mxq(f64(head_weight), 0, "e4m3"))
    h = xq @ mxq(f64(tail_proj_0), 0, "e4m3")
    tail_sm = softmax(mxq(h, 2, "e4m3") @ mxq(f64(tail_w_0), 0, "e4m3"))
    probs = np.concatenate([head_sm[..., :B0], tail_sm * head_sm[..., B0:B0 + 1]], axis=-1)
    return probs, head_sm[..., B0 + 1:B0 + C]

@@ -1,0 +1,321 @@
+from contextlib import ExitStack
+
+import concourse.mybir as mybir
+from concourse.masks import make_identity
+
+F32 = mybir.dt.float32
+BF16 = mybir.dt.bfloat16
+U32 = mybir.dt.uint32
+U8 = mybir.dt.uint8
+FP8X4 = mybir.dt.float8_e4m3fn_x4
+ALU = mybir.AluOpType
+ACT = mybir.ActivationFunctionType
+AX = mybir.AxisListType
+
+P = 128
+TOKENS = 1024
+D = 1024
+V = 2048
+P0 = 512
+NT = TOKENS // P
+HEAD_TOKENS = 2046
+BANK = 512
+LAST_SPLIT = 1344
+
+FLOPS = 2 * TOKENS * (D * V + D * P0 + P0 * V)
+
+
+def tile_adaptiveinputsoftmax_pa_kernel(tc, x, head_weight, tail_proj_0, tail_w_0, out_0, out_1):
+    nc = tc.nc
+    xf = x.flatten_outer_dims()
+    o0 = out_0.flatten_outer_dims()
+    o1 = out_1.flatten_outer_dims()
+
+    with ExitStack() as ctx:
+        ctx.enter_context(tc.manual_schedule())
+        keep = ctx.enter_context(tc.tile_pool(name="keep", bufs=1))
+        gwp = ctx.enter_context(tc.tile_pool(name="gwp", bufs=5))
+        epool = ctx.enter_context(tc.tile_pool(name="epool", bufs=6))
+        stats = ctx.enter_context(tc.tile_pool(name="stats", bufs=4))
+        psum = ctx.enter_context(tc.psum_pool(name="psum", bufs=8))
+
+        tp_raw = keep.tile([P, 2, 4, P0], BF16)
+        for g in range(2):
+            nc.sync.dma_start(
+                out=tp_raw[:, g, :, :].rearrange("p (u e) c -> p u (e c)", u=2),
+                in_=tail_proj_0[512 * g : 512 * g + 512, :].rearrange("(u q e) c -> q u (e c)", u=2, e=2),
+            )
+        hw_raw = keep.tile([P, 2, 4, V], BF16)
+        for g in range(2):
+            for hf in range(2):
+                for u in range(2):
+                    r0 = 512 * g + 256 * u
+                    nc.sync.dma_start(
+                        out=hw_raw[:, g, 2 * u : 2 * u + 2, 1024 * hf : 1024 * hf + 1024],
+                        in_=head_weight[r0 : r0 + 256, 1024 * hf : 1024 * hf + 1024].rearrange(
+                            "(q e) c -> q e c", e=2
+                        ),
+                    )
+        x_raw = keep.tile([P, NT, D], BF16)
+        for a in range(4):
+            nc.sync.dma_start(
+                out=x_raw[:, 2 * a : 2 * a + 2, :],
+                in_=xf[256 * a : 256 * a + 256, :].rearrange("(i p) k -> p i k", p=P),
+            )
+        tw_raw = keep.tile([P, 4, V], BF16)
+        for hf in range(2):
+            nc.sync.dma_start(
+                out=tw_raw[:, :, 1024 * hf : 1024 * hf + 1024],
+                in_=tail_w_0[:, 1024 * hf : 1024 * hf + 1024].rearrange("(t p) n -> p t n", p=P),
+            )
+
+        warm_in = keep.tile([P, 1], F32)
+        warm_out = keep.tile([P, 1], F32)
+        nc.vector.memset(warm_in[:], 0.0)
+        nc.scalar.activation(out=warm_out[:], in_=warm_in[:], func=ACT.Exp)
+        cl = keep.tile([P, 2, P], F32)
+        nc.vector.memset(cl[:], 0.0)
+        ident = keep.tile([P, P], F32)
+        make_identity(nc, ident[:])
+
+        x_codes = keep.tile([P, NT, 2 * P], U32, align_bytes=64)
+        x_scales = keep.tile([P, NT, 2 * P], U8, align_bytes=64)
+        tp_codes = keep.tile([P, 2, P0], U32, align_bytes=64)
+        tp_scales = keep.tile([P, 2, P0], U8, align_bytes=64)
+        hw_codes = keep.tile([P, 2, V], U32, align_bytes=64)
+        hw_scales = keep.tile([P, 2, V], U8, align_bytes=64)
+        tw_codes = keep.tile([P, V], U32, align_bytes=64)
+        tw_scales = keep.tile([P, V], U8, align_bytes=64)
+        gx = keep.tile([P, NT, 2, P, 2], F32, align_bytes=64)
+        gh = keep.tile([P, NT, P, 4], BF16, align_bytes=64)
+        h_codes = keep.tile([P, NT * P], U32, align_bytes=64)
+        h_scales = keep.tile([P, NT * P], U8, align_bytes=64)
+
+        units = {}
+        for g in range(2):
+            units["A%d" % g] = (tp_raw[:, g, :, :], tp_codes[:, g, :], tp_scales[:, g, :])
+        for n in range(8):
+            g, c = divmod(n, 4)
+            cols = slice(BANK * c, BANK * c + BANK)
+            units["B%d" % n] = (hw_raw[:, g, :, cols], hw_codes[:, g, cols], hw_scales[:, g, cols])
+        for c in range(4):
+            cols = slice(BANK * c, BANK * c + BANK)
+            units["C%d" % c] = (tw_raw[:, :, cols], tw_codes[:, cols], tw_scales[:, cols])
+        grouped = {}
+
+        def regroup(u, on_scalar):
+            gw = gwp.tile([P, BANK, 4], BF16, align_bytes=64, name="gw")
+            grouped[u] = gw
+            dst_v = gw[:].rearrange("p (c i) t -> p c t i", i=4)
+            src_v = units[u][0].rearrange("p t (c i) -> p c t i", i=4)
+            if on_scalar:
+                nc.scalar.copy(out=dst_v, in_=src_v)
+            else:
+                nc.vector.tensor_copy(out=dst_v, in_=src_v)
+
+        def quantise(u):
+            nc.vector.quantize_mx(
+                out=units[u][1].bitcast(FP8X4),
+                scales=units[u][2],
+                in_=grouped[u][:].rearrange("p w t -> p (w t)"),
+            )
+
+        banks = {}
+
+        def new_bank(key):
+            bank = psum.tile([P, BANK], F32, tag="bank", name="bank")
+            banks[key] = bank
+            return bank
+
+        def x_transpose(i):
+            xw = x_raw[:, i, :].bitcast(F32)
+            bank = new_bank(("x", i))
+            for c in range(4):
+                nc.tensor.transpose(bank[:, P * c : P * c + P], xw[:, P * c : P * c + P], ident[:])
+
+        def x_out(i):
+            nc.scalar.copy(
+                out=gx[:, i, :, :, :], in_=banks[("x", i)][:].rearrange("p (g u r) -> p g r u", g=2, u=2)
+            )
+
+        def x_quantise(i):
+            nc.vector.quantize_mx(
+                out=x_codes[:, i, :].bitcast(FP8X4),
+                scales=x_scales[:, i, :],
+                in_=gx[:, i, :, :, :].rearrange("p g r u -> p (g r u)").bitcast(BF16),
+            )
+
+        def h_matmuls(i):
+            bank = new_bank(("h", i))
+            for j in range(4):
+                for g in range(2):
+                    nc.tensor.matmul_mx(
+                        out=bank[:, P * j : P * j + P],
+                        lhsT=tp_codes[:, g, P * j : P * j + P].bitcast(FP8X4),
+                        lhsT_scale=tp_scales[:, g, P * j : P * j + P],
+                        rhs=x_codes[:, i, P * g : P * g + P].bitcast(FP8X4),
+                        rhs_scale=x_scales[:, i, P * g : P * g + P],
+                        start=(g == 0),
+                        stop=(g == 1),
+                    )
+
+        def h_out(i):
+            nc.scalar.copy(out=gh[:, i, :, :], in_=banks[("h", i)][:].rearrange("p (j r) -> p r j", j=4))
+
+        def h_quantise(a):
+            nc.vector.quantize_mx(
+                out=h_codes[:, 512 * a : 512 * a + 512].bitcast(FP8X4),
+                scales=h_scales[:, 512 * a : 512 * a + 512],
+                in_=gh[:, 4 * a : 4 * a + 4, :, :].rearrange("p i r j -> p (i r j)"),
+            )
+
+        def logits(n):
+            i = n % NT
+            for c in range(4):
+                cols = slice(BANK * c, BANK * c + BANK)
+                bank = new_bank((n, c))
+                if n < NT:
+                    for g in range(2):
+                        nc.tensor.matmul_mx(
+                            out=bank[:],
+                            lhsT=x_codes[:, i, P * g : P * g + P].bitcast(FP8X4),
+                            lhsT_scale=x_scales[:, i, P * g : P * g + P],
+                            rhs=hw_codes[:, g, cols].bitcast(FP8X4),
+                            rhs_scale=hw_scales[:, g, cols],
+                            start=(g == 0),
+                            stop=(g == 1),
+                        )
+                else:
+                    nc.tensor.matmul_mx(
+                        out=bank[:],
+                        lhsT=h_codes[:, P * i : P * i + P].bitcast(FP8X4),
+                        lhsT_scale=h_scales[:, P * i : P * i + P],
+                        rhs=tw_codes[:, cols].bitcast(FP8X4),
+                        rhs_scale=tw_scales[:, cols],
+                        start=True,
+                        stop=True,
+                    )
+
+        small = {}
+
+        def row_max(n):
+            m4 = stats.tile([P, 4], F32, name="m4")
+            for c in range(4):
+                nc.vector.tensor_reduce(out=m4[:, c : c + 1], in_=banks[(n, c)][:], axis=AX.X, op=ALU.max)
+            negm = stats.tile([P, 1], F32, name="negm")
+            nc.vector.tensor_reduce(out=negm[:], in_=m4[:], axis=AX.X, op=ALU.max, negate=True)
+            small[("negm", n)] = negm
+
+        def exps(n):
+            e = epool.tile([P, V], F32, name="e")
+            s4 = stats.tile([P, 4], F32, name="s4")
+            small[("e", n)] = e
+            small[("s4", n)] = s4
+            for c in range(4):
+                nc.scalar.activation(
+                    out=e[:, BANK * c : BANK * c + BANK],
+                    in_=banks[(n, c)][:],
+                    func=ACT.Exp,
+                    bias=small[("negm", n)][:, 0:1],
+                    scale=1.0,
+                    accum_out=s4[:, c : c + 1],
+                )
+
+        def finish(n):
+            i = n % NT
+            rows = slice(P * i, P * i + P)
+            e = small[("e", n)]
+            s = stats.tile([P, 1], F32, name="s")
+            nc.vector.tensor_reduce(out=s[:], in_=small[("s4", n)][:], axis=AX.X, op=ALU.add)
+            r = stats.tile([P, 1], F32, name="r")
+            nc.vector.reciprocal(out=r[:], in_=s[:])
+            if n < NT:
+                nc.gpsimd.tensor_scalar(
+                    out=cl[:, :, i], in0=e[:, HEAD_TOKENS:V], scalar1=r[:, 0:1], scalar2=0.0,
+                    op0=ALU.mult, op1=ALU.add,
+                )
+                nc.gpsimd.tensor_scalar(
+                    out=e[:, 0:HEAD_TOKENS], in0=e[:, 0:HEAD_TOKENS],
+                    scalar1=r[:, 0:1], scalar2=0.0, op0=ALU.mult, op1=ALU.add,
+                )
+                nc.sync.dma_start(out=o0[rows, 0:HEAD_TOKENS], in_=e[:, 0:HEAD_TOKENS])
+            elif n < 2 * NT - 2:
+                nc.gpsimd.tensor_scalar(
+                    out=e[:], in0=e[:],
+                    scalar1=r[:, 0:1], scalar2=cl[:, 0, i : i + 1], op0=ALU.mult, op1=ALU.mult,
+                )
+                nc.sync.dma_start(out=o0[rows, HEAD_TOKENS : HEAD_TOKENS + V], in_=e[:])
+            elif n == 2 * NT - 2:
+                for hf in range(2):
+                    cols = slice(1024 * hf, 1024 * hf + 1024)
+                    nc.gpsimd.tensor_scalar(
+                        out=e[:, cols], in0=e[:, cols],
+                        scalar1=r[:, 0:1], scalar2=cl[:, 0, i : i + 1], op0=ALU.mult, op1=ALU.mult,
+                    )
+                    nc.sync.dma_start(
+                        out=o0[rows, HEAD_TOKENS + 1024 * hf : HEAD_TOKENS + 1024 * hf + 1024], in_=e[:, cols]
+                    )
+            else:
+                rc = stats.tile([P, 1], F32, name="rc")
+                nc.vector.tensor_scalar(
+                    out=rc[:], in0=r[:], scalar1=cl[:, 0, i : i + 1], scalar2=None, op0=ALU.mult
+                )
+                nc.vector.tensor_scalar(
+                    out=e[:, 0:LAST_SPLIT], in0=e[:, 0:LAST_SPLIT], scalar1=rc[:, 0:1], scalar2=None, op0=ALU.mult
+                )
+                nc.scalar.activation(
+                    out=e[:, LAST_SPLIT:V], in_=e[:, LAST_SPLIT:V], func=ACT.Copy, scale=rc[:, 0:1]
+                )
+                nc.sync.dma_start(out=o0[rows, HEAD_TOKENS : HEAD_TOKENS + LAST_SPLIT], in_=e[:, 0:LAST_SPLIT])
+                nc.sync.dma_start(out=o0[rows, HEAD_TOKENS + LAST_SPLIT : HEAD_TOKENS + V], in_=e[:, LAST_SPLIT:V])
+
+        first = ["A0", "A1", "B0", "B1", "B2", "B3", "B4", "B5", "B6", "B7"]
+        for k in range(5):
+            regroup(first[2 * k + 1], True)
+            regroup(first[2 * k], False)
+            if k > 0:
+                quantise(first[2 * k - 1])
+            quantise(first[2 * k])
+        for i in range(NT):
+            x_transpose(i)
+        for i in range(NT):
+            x_out(i)
+        quantise("B7")
+        for i in range(NT):
+            x_quantise(i)
+        logits(0)
+        logits(1)
+        regroup("C1", True)
+        regroup("C0", False)
+        row_max(0)
+        quantise("C0")
+        regroup("C3", True)
+        regroup("C2", False)
+        quantise("C1")
+        row_max(1)
+        quantise("C2")
+        quantise("C3")
+
+        h_tiles = {1: (0, 1), 2: (2, 3), 3: (4, 5), 4: (6, 7)}
+        for n in range(2 * NT):
+            if 1 <= n < 2 * NT - 1:
+                logits(n + 1)
+            exps(n)
+            for i in h_tiles.get(n, ()):
+                h_matmuls(i)
+            for i in h_tiles.get(n, ()):
+                h_out(i)
+            if n == 9:
+                o1_bank = new_bank("o1")
+                nc.tensor.transpose(o1_bank[:, 0:P], cl[:, 1, :], ident[:])
+            if 1 <= n < 2 * NT - 1:
+                row_max(n + 1)
+            if n == 3:
+                h_quantise(0)
+            if n == 5:
+                h_quantise(1)
+            if n == 9:
+                o1_sb = keep.tile([P, P], F32)
+                nc.vector.tensor_copy(out=o1_sb[:], in_=banks["o1"][:, 0:P])
+                nc.sync.dma_start(out=o1.rearrange("(i p) o -> i (p o)", p=P), in_=o1_sb[0:NT, :])
+            finish(n)

@@ -198,13 +198,23 @@ def tile_adaptiveinputsoftmax_pa_kernel(tc, x, head_weight, tail_proj_0, tail_w_
 
         small = {}
 
-        def row_max(n):
-            m4 = stats.tile([P, 4], F32, name="m4")
-            for c in range(4):
-                nc.vector.tensor_reduce(out=m4[:, c : c + 1], in_=banks[(n, c)][:], axis=AX.X, op=ALU.max)
+        def bank_max(n, chunks):
+            if ("m4", n) not in small:
+                m4 = stats.tile([P, 4], F32, name="m4")
+                small[("m4", n)] = m4
+            for c in chunks:
+                nc.vector.tensor_reduce(
+                    out=small[("m4", n)][:, c : c + 1], in_=banks[(n, c)][:], axis=AX.X, op=ALU.max
+                )
+
+        def set_max(n):
             negm = stats.tile([P, 1], F32, name="negm")
-            nc.vector.tensor_reduce(out=negm[:], in_=m4[:], axis=AX.X, op=ALU.max, negate=True)
+            nc.vector.tensor_reduce(out=negm[:], in_=small[("m4", n)][:], axis=AX.X, op=ALU.max, negate=True)
             small[("negm", n)] = negm
+
+        def row_max(n):
+            bank_max(n, (0, 1, 2, 3))
+            set_max(n)
 
         def exps(n):
             e = epool.tile([P, V], F32, name="e")
@@ -298,24 +308,30 @@ def tile_adaptiveinputsoftmax_pa_kernel(tc, x, head_weight, tail_proj_0, tail_w_
 
         h_tiles = {1: (0, 1), 2: (2, 3), 3: (4, 5), 4: (6, 7)}
         for n in range(2 * NT):
-            if 1 <= n < 2 * NT - 1:
+            ahead = 1 <= n < 2 * NT - 1
+            if ahead:
                 logits(n + 1)
             exps(n)
             for i in h_tiles.get(n, ()):
                 h_matmuls(i)
             for i in h_tiles.get(n, ()):
                 h_out(i)
-            if n == 9:
+            if n == 11:
                 o1_bank = new_bank("o1")
                 nc.tensor.transpose(o1_bank[:, 0:P], cl[:, 1, :], ident[:])
-            if 1 <= n < 2 * NT - 1:
-                row_max(n + 1)
+            if ahead:
+                bank_max(n + 1, (0, 1))
             if n == 3:
                 h_quantise(0)
             if n == 5:
                 h_quantise(1)
-            if n == 9:
+            if n == 11:
                 o1_sb = keep.tile([P, P], F32)
                 nc.vector.tensor_copy(out=o1_sb[:], in_=banks["o1"][:, 0:P])
                 nc.sync.dma_start(out=o1.rearrange("(i p) o -> i (p o)", p=P), in_=o1_sb[0:NT, :])
-            finish(n)
+            if n >= 1:
+                finish(n - 1)
+            if ahead:
+                bank_max(n + 1, (2, 3))
+                set_max(n + 1)
+        finish(2 * NT - 1)

@@ -34,7 +34,7 @@ def tile_adaptiveinputsoftmax_pa_kernel(tc, x, head_weight, tail_proj_0, tail_w_
     with ExitStack() as ctx:
         ctx.enter_context(tc.manual_schedule())
         keep = ctx.enter_context(tc.tile_pool(name="keep", bufs=1))
-        gwp = ctx.enter_context(tc.tile_pool(name="gwp", bufs=5))
+        gwp = ctx.enter_context(tc.tile_pool(name="gwp", bufs=4))
         epool = ctx.enter_context(tc.tile_pool(name="epool", bufs=6))
         stats = ctx.enter_context(tc.tile_pool(name="stats", bufs=4))
         psum = ctx.enter_context(tc.psum_pool(name="psum", bufs=8))
@@ -88,6 +88,7 @@ def tile_adaptiveinputsoftmax_pa_kernel(tc, x, head_weight, tail_proj_0, tail_w_
         tw_scales = keep.tile([P, V], U8, align_bytes=64)
         gx = keep.tile([P, NT, 2, P, 2], F32, align_bytes=64)
         gh = keep.tile([P, NT, P, 4], BF16, align_bytes=64)
+        gc = keep.tile([P, 4, BANK, 4], BF16, align_bytes=64)
         h_codes = keep.tile([P, NT * P], U32, align_bytes=64)
         h_scales = keep.tile([P, NT * P], U8, align_bytes=64)
 
@@ -98,9 +99,6 @@ def tile_adaptiveinputsoftmax_pa_kernel(tc, x, head_weight, tail_proj_0, tail_w_
             g, c = divmod(n, 4)
             cols = slice(BANK * c, BANK * c + BANK)
             units["B%d" % n] = (hw_raw[:, g, :, cols], hw_codes[:, g, cols], hw_scales[:, g, cols])
-        for c in range(4):
-            cols = slice(BANK * c, BANK * c + BANK)
-            units["C%d" % c] = (tw_raw[:, :, cols], tw_codes[:, cols], tw_scales[:, cols])
         grouped = {}
 
         def regroup(u, on_scalar):
@@ -118,6 +116,20 @@ def tile_adaptiveinputsoftmax_pa_kernel(tc, x, head_weight, tail_proj_0, tail_w_
                 out=units[u][1].bitcast(FP8X4),
                 scales=units[u][2],
                 in_=grouped[u][:].rearrange("p w t -> p (w t)"),
+            )
+
+        def tw_regroup(c):
+            nc.gpsimd.tensor_scalar(
+                out=gc[:, c, :, :],
+                in0=tw_raw[:, :, BANK * c : BANK * c + BANK].rearrange("p t w -> p w t"),
+                scalar1=1.0, scalar2=0.0, op0=ALU.mult, op1=ALU.add,
+            )
+
+        def tw_quantise(a):
+            nc.vector.quantize_mx(
+                out=tw_codes[:, 1024 * a : 1024 * a + 1024].bitcast(FP8X4),
+                scales=tw_scales[:, 1024 * a : 1024 * a + 1024],
+                in_=gc[:, 2 * a : 2 * a + 2, :, :].rearrange("p c w t -> p (c w t)"),
             )
 
         banks = {}
@@ -198,23 +210,13 @@ def tile_adaptiveinputsoftmax_pa_kernel(tc, x, head_weight, tail_proj_0, tail_w_
 
         small = {}
 
-        def bank_max(n, chunks):
-            if ("m4", n) not in small:
-                m4 = stats.tile([P, 4], F32, name="m4")
-                small[("m4", n)] = m4
-            for c in chunks:
-                nc.vector.tensor_reduce(
-                    out=small[("m4", n)][:, c : c + 1], in_=banks[(n, c)][:], axis=AX.X, op=ALU.max
-                )
-
-        def set_max(n):
-            negm = stats.tile([P, 1], F32, name="negm")
-            nc.vector.tensor_reduce(out=negm[:], in_=small[("m4", n)][:], axis=AX.X, op=ALU.max, negate=True)
-            small[("negm", n)] = negm
-
         def row_max(n):
-            bank_max(n, (0, 1, 2, 3))
-            set_max(n)
+            m4 = stats.tile([P, 4], F32, name="m4")
+            for c in range(4):
+                nc.vector.tensor_reduce(out=m4[:, c : c + 1], in_=banks[(n, c)][:], axis=AX.X, op=ALU.max)
+            negm = stats.tile([P, 1], F32, name="negm")
+            nc.vector.tensor_reduce(out=negm[:], in_=m4[:], axis=AX.X, op=ALU.max, negate=True)
+            small[("negm", n)] = negm
 
         def exps(n):
             e = epool.tile([P, V], F32, name="e")
@@ -258,7 +260,7 @@ def tile_adaptiveinputsoftmax_pa_kernel(tc, x, head_weight, tail_proj_0, tail_w_
             elif n == 2 * NT - 2:
                 for hf in range(2):
                     cols = slice(1024 * hf, 1024 * hf + 1024)
-                    nc.gpsimd.tensor_scalar(
+                    nc.vector.tensor_scalar(
                         out=e[:, cols], in0=e[:, cols],
                         scalar1=r[:, 0:1], scalar2=cl[:, 0, i : i + 1], op0=ALU.mult, op1=ALU.mult,
                     )
@@ -286,52 +288,51 @@ def tile_adaptiveinputsoftmax_pa_kernel(tc, x, head_weight, tail_proj_0, tail_w_
             if k > 0:
                 quantise(first[2 * k - 1])
             quantise(first[2 * k])
-        for i in range(NT):
+        for c in range(4):
+            tw_regroup(c)
+        for i in range(4):
             x_transpose(i)
-        for i in range(NT):
+        for i in range(4):
             x_out(i)
         quantise("B7")
-        for i in range(NT):
-            x_quantise(i)
+        x_quantise(0)
         logits(0)
-        logits(1)
-        regroup("C1", True)
-        regroup("C0", False)
+        for i in range(4, NT):
+            x_transpose(i)
+        for i in range(4, NT):
+            x_out(i)
+        for i in range(1, 4):
+            x_quantise(i)
         row_max(0)
-        quantise("C0")
-        regroup("C3", True)
-        regroup("C2", False)
-        quantise("C1")
+        logits(1)
+        for i in range(4, NT):
+            x_quantise(i)
         row_max(1)
-        quantise("C2")
-        quantise("C3")
 
         h_tiles = {1: (0, 1), 2: (2, 3), 3: (4, 5), 4: (6, 7)}
         for n in range(2 * NT):
-            ahead = 1 <= n < 2 * NT - 1
-            if ahead:
+            if 1 <= n < 2 * NT - 1:
                 logits(n + 1)
             exps(n)
             for i in h_tiles.get(n, ()):
                 h_matmuls(i)
             for i in h_tiles.get(n, ()):
                 h_out(i)
-            if n == 11:
+            if n == 12:
                 o1_bank = new_bank("o1")
                 nc.tensor.transpose(o1_bank[:, 0:P], cl[:, 1, :], ident[:])
-            if ahead:
-                bank_max(n + 1, (0, 1))
+            if 1 <= n < 2 * NT - 1:
+                row_max(n + 1)
             if n == 3:
                 h_quantise(0)
+            if n == 4:
+                tw_quantise(0)
             if n == 5:
                 h_quantise(1)
-            if n == 11:
+            if n == 6:
+                tw_quantise(1)
+            if n == 12:
                 o1_sb = keep.tile([P, P], F32)
                 nc.vector.tensor_copy(out=o1_sb[:], in_=banks["o1"][:, 0:P])
                 nc.sync.dma_start(out=o1.rearrange("(i p) o -> i (p o)", p=P), in_=o1_sb[0:NT, :])
-            if n >= 1:
-                finish(n - 1)
-            if ahead:
-                bank_max(n + 1, (2, 3))
-                set_max(n + 1)
-        finish(2 * NT - 1)
+            finish(n)

@@ -21,6 +21,7 @@ NT = TOKENS // P
 HEAD_TOKENS = 2046
 BANK = 512
 LAST_SPLIT = 1344
+BIG_BUFS = 13
 
 FLOPS = 2 * TOKENS * (D * V + D * P0 + P0 * V)
 
@@ -34,38 +35,46 @@ def tile_adaptiveinputsoftmax_pa_kernel(tc, x, head_weight, tail_proj_0, tail_w_
     with ExitStack() as ctx:
         ctx.enter_context(tc.manual_schedule())
         keep = ctx.enter_context(tc.tile_pool(name="keep", bufs=1))
-        gwp = ctx.enter_context(tc.tile_pool(name="gwp", bufs=4))
-        epool = ctx.enter_context(tc.tile_pool(name="epool", bufs=6))
+        gwp = ctx.enter_context(tc.tile_pool(name="gwp", bufs=5))
+        big = ctx.enter_context(tc.tile_pool(name="big", bufs=BIG_BUFS))
         stats = ctx.enter_context(tc.tile_pool(name="stats", bufs=4))
         psum = ctx.enter_context(tc.psum_pool(name="psum", bufs=8))
 
-        tp_raw = keep.tile([P, 2, 4, P0], BF16)
+        tp_raw = big.tile([P, 2, 4, P0], BF16, tag="big", name="tp_raw")
         for g in range(2):
             nc.sync.dma_start(
                 out=tp_raw[:, g, :, :].rearrange("p (u e) c -> p u (e c)", u=2),
                 in_=tail_proj_0[512 * g : 512 * g + 512, :].rearrange("(u q e) c -> q u (e c)", u=2, e=2),
             )
-        hw_raw = keep.tile([P, 2, 4, V], BF16)
+        hw_raw = {}
         for g in range(2):
             for hf in range(2):
+                hw_part = big.tile([P, 4, 1024], BF16, tag="big", name="hw_part")
+                hw_raw[(g, hf)] = hw_part
                 for u in range(2):
                     r0 = 512 * g + 256 * u
                     nc.sync.dma_start(
-                        out=hw_raw[:, g, 2 * u : 2 * u + 2, 1024 * hf : 1024 * hf + 1024],
+                        out=hw_part[:, 2 * u : 2 * u + 2, :],
                         in_=head_weight[r0 : r0 + 256, 1024 * hf : 1024 * hf + 1024].rearrange(
                             "(q e) c -> q e c", e=2
                         ),
                     )
-        x_raw = keep.tile([P, NT, D], BF16)
-        for a in range(4):
-            nc.sync.dma_start(
-                out=x_raw[:, 2 * a : 2 * a + 2, :],
-                in_=xf[256 * a : 256 * a + 256, :].rearrange("(i p) k -> p i k", p=P),
-            )
-        tw_raw = keep.tile([P, 4, V], BF16)
+        x_raw = {}
+        for b in range(2):
+            x_part = big.tile([P, 4, D], BF16, tag="big", name="x_part")
+            x_raw[b] = x_part
+            for a in range(2):
+                t0 = 512 * b + 256 * a
+                nc.sync.dma_start(
+                    out=x_part[:, 2 * a : 2 * a + 2, :],
+                    in_=xf[t0 : t0 + 256, :].rearrange("(i p) k -> p i k", p=P),
+                )
+        tw_raw = {}
         for hf in range(2):
+            tw_part = big.tile([P, 4, 1024], BF16, tag="big", name="tw_part")
+            tw_raw[hf] = tw_part
             nc.sync.dma_start(
-                out=tw_raw[:, :, 1024 * hf : 1024 * hf + 1024],
+                out=tw_part[:],
                 in_=tail_w_0[:, 1024 * hf : 1024 * hf + 1024].rearrange("(t p) n -> p t n", p=P),
             )
 
@@ -88,7 +97,6 @@ def tile_adaptiveinputsoftmax_pa_kernel(tc, x, head_weight, tail_proj_0, tail_w_
         tw_scales = keep.tile([P, V], U8, align_bytes=64)
         gx = keep.tile([P, NT, 2, P, 2], F32, align_bytes=64)
         gh = keep.tile([P, NT, P, 4], BF16, align_bytes=64)
-        gc = keep.tile([P, 4, BANK, 4], BF16, align_bytes=64)
         h_codes = keep.tile([P, NT * P], U32, align_bytes=64)
         h_scales = keep.tile([P, NT * P], U8, align_bytes=64)
 
@@ -98,7 +106,12 @@ def tile_adaptiveinputsoftmax_pa_kernel(tc, x, head_weight, tail_proj_0, tail_w_
         for n in range(8):
             g, c = divmod(n, 4)
             cols = slice(BANK * c, BANK * c + BANK)
-            units["B%d" % n] = (hw_raw[:, g, :, cols], hw_codes[:, g, cols], hw_scales[:, g, cols])
+            part = slice(BANK * (c % 2), BANK * (c % 2) + BANK)
+            units["B%d" % n] = (hw_raw[(g, c // 2)][:, :, part], hw_codes[:, g, cols], hw_scales[:, g, cols])
+        for c in range(4):
+            cols = slice(BANK * c, BANK * c + BANK)
+            part = slice(BANK * (c % 2), BANK * (c % 2) + BANK)
+            units["C%d" % c] = (tw_raw[c // 2][:, :, part], tw_codes[:, cols], tw_scales[:, cols])
         grouped = {}
 
         def regroup(u, on_scalar):
@@ -118,20 +131,6 @@ def tile_adaptiveinputsoftmax_pa_kernel(tc, x, head_weight, tail_proj_0, tail_w_
                 in_=grouped[u][:].rearrange("p w t -> p (w t)"),
             )
 
-        def tw_regroup(c):
-            nc.gpsimd.tensor_scalar(
-                out=gc[:, c, :, :],
-                in0=tw_raw[:, :, BANK * c : BANK * c + BANK].rearrange("p t w -> p w t"),
-                scalar1=1.0, scalar2=0.0, op0=ALU.mult, op1=ALU.add,
-            )
-
-        def tw_quantise(a):
-            nc.vector.quantize_mx(
-                out=tw_codes[:, 1024 * a : 1024 * a + 1024].bitcast(FP8X4),
-                scales=tw_scales[:, 1024 * a : 1024 * a + 1024],
-                in_=gc[:, 2 * a : 2 * a + 2, :, :].rearrange("p c w t -> p (c w t)"),
-            )
-
         banks = {}
 
         def new_bank(key):
@@ -140,7 +139,7 @@ def tile_adaptiveinputsoftmax_pa_kernel(tc, x, head_weight, tail_proj_0, tail_w_
             return bank
 
         def x_transpose(i):
-            xw = x_raw[:, i, :].bitcast(F32)
+            xw = x_raw[i // 4][:, i % 4, :].bitcast(F32)
             bank = new_bank(("x", i))
             for c in range(4):
                 nc.tensor.transpose(bank[:, P * c : P * c + P], xw[:, P * c : P * c + P], ident[:])
@@ -219,7 +218,7 @@ def tile_adaptiveinputsoftmax_pa_kernel(tc, x, head_weight, tail_proj_0, tail_w_
             small[("negm", n)] = negm
 
         def exps(n):
-            e = epool.tile([P, V], F32, name="e")
+            e = big.tile([P, V], F32, tag="big", name="e")
             s4 = stats.tile([P, 4], F32, name="s4")
             small[("e", n)] = e
             small[("s4", n)] = s4
@@ -260,7 +259,7 @@ def tile_adaptiveinputsoftmax_pa_kernel(tc, x, head_weight, tail_proj_0, tail_w_
             elif n == 2 * NT - 2:
                 for hf in range(2):
                     cols = slice(1024 * hf, 1024 * hf + 1024)
-                    nc.vector.tensor_scalar(
+                    nc.gpsimd.tensor_scalar(
                         out=e[:, cols], in0=e[:, cols],
                         scalar1=r[:, 0:1], scalar2=cl[:, 0, i : i + 1], op0=ALU.mult, op1=ALU.mult,
                     )
@@ -288,26 +287,25 @@ def tile_adaptiveinputsoftmax_pa_kernel(tc, x, head_weight, tail_proj_0, tail_w_
             if k > 0:
                 quantise(first[2 * k - 1])
             quantise(first[2 * k])
-        for c in range(4):
-            tw_regroup(c)
-        for i in range(4):
+        for i in range(NT):
             x_transpose(i)
-        for i in range(4):
+        for i in range(NT):
             x_out(i)
         quantise("B7")
-        x_quantise(0)
+        for i in range(NT):
+            x_quantise(i)
         logits(0)
-        for i in range(4, NT):
-            x_transpose(i)
-        for i in range(4, NT):
-            x_out(i)
-        for i in range(1, 4):
-            x_quantise(i)
-        row_max(0)
         logits(1)
-        for i in range(4, NT):
-            x_quantise(i)
+        regroup("C1", True)
+        regroup("C0", False)
+        row_max(0)
+        quantise("C0")
+        regroup("C3", True)
+        regroup("C2", False)
+        quantise("C1")
         row_max(1)
+        quantise("C2")
+        quantise("C3")
 
         h_tiles = {1: (0, 1), 2: (2, 3), 3: (4, 5), 4: (6, 7)}
         for n in range(2 * NT):
@@ -318,20 +316,16 @@ def tile_adaptiveinputsoftmax_pa_kernel(tc, x, head_weight, tail_proj_0, tail_w_
                 h_matmuls(i)
             for i in h_tiles.get(n, ()):
                 h_out(i)
-            if n == 12:
+            if n == 9:
                 o1_bank = new_bank("o1")
                 nc.tensor.transpose(o1_bank[:, 0:P], cl[:, 1, :], ident[:])
             if 1 <= n < 2 * NT - 1:
                 row_max(n + 1)
             if n == 3:
                 h_quantise(0)
-            if n == 4:
-                tw_quantise(0)
             if n == 5:
                 h_quantise(1)
-            if n == 6:
-                tw_quantise(1)
-            if n == 12:
+            if n == 9:
                 o1_sb = keep.tile([P, P], F32)
                 nc.vector.tensor_copy(out=o1_sb[:], in_=banks["o1"][:, 0:P])
                 nc.sync.dma_start(out=o1.rearrange("(i p) o -> i (p o)", p=P), in_=o1_sb[0:NT, :])

@@ -209,13 +209,23 @@ def tile_adaptiveinputsoftmax_pa_kernel(tc, x, head_weight, tail_proj_0, tail_w_
 
         small = {}
 
-        def row_max(n):
-            m4 = stats.tile([P, 4], F32, name="m4")
-            for c in range(4):
-                nc.vector.tensor_reduce(out=m4[:, c : c + 1], in_=banks[(n, c)][:], axis=AX.X, op=ALU.max)
+        def bank_max(n, chunks):
+            if ("m4", n) not in small:
+                m4 = stats.tile([P, 4], F32, name="m4")
+                small[("m4", n)] = m4
+            for c in chunks:
+                nc.vector.tensor_reduce(
+                    out=small[("m4", n)][:, c : c + 1], in_=banks[(n, c)][:], axis=AX.X, op=ALU.max
+                )
+
+        def set_max(n):
             negm = stats.tile([P, 1], F32, name="negm")
-            nc.vector.tensor_reduce(out=negm[:], in_=m4[:], axis=AX.X, op=ALU.max, negate=True)
+            nc.vector.tensor_reduce(out=negm[:], in_=small[("m4", n)][:], axis=AX.X, op=ALU.max, negate=True)
             small[("negm", n)] = negm
+
+        def row_max(n):
+            bank_max(n, (0, 1, 2, 3))
+            set_max(n)
 
         def exps(n):
             e = big.tile([P, V], F32, tag="big", name="e")
@@ -295,37 +305,42 @@ def tile_adaptiveinputsoftmax_pa_kernel(tc, x, head_weight, tail_proj_0, tail_w_
         for i in range(NT):
             x_quantise(i)
         logits(0)
-        logits(1)
         regroup("C1", True)
         regroup("C0", False)
-        row_max(0)
+        for i in range(4):
+            h_matmuls(i)
+        bank_max(0, (0, 1))
         quantise("C0")
         regroup("C3", True)
         regroup("C2", False)
         quantise("C1")
-        row_max(1)
+        for i in range(4):
+            h_out(i)
+        bank_max(0, (2, 3))
+        set_max(0)
         quantise("C2")
         quantise("C3")
+        for i in range(4, NT):
+            h_matmuls(i)
+        for i in range(4, NT):
+            h_out(i)
+        h_quantise(0)
+        logits(1)
+        bank_max(1, (0, 1))
+        h_quantise(1)
+        bank_max(1, (2, 3))
+        set_max(1)
 
-        h_tiles = {1: (0, 1), 2: (2, 3), 3: (4, 5), 4: (6, 7)}
         for n in range(2 * NT):
             if 1 <= n < 2 * NT - 1:
                 logits(n + 1)
             exps(n)
-            for i in h_tiles.get(n, ()):
-                h_matmuls(i)
-            for i in h_tiles.get(n, ()):
-                h_out(i)
-            if n == 9:
+            if n == 10:
                 o1_bank = new_bank("o1")
                 nc.tensor.transpose(o1_bank[:, 0:P], cl[:, 1, :], ident[:])
             if 1 <= n < 2 * NT - 1:
                 row_max(n + 1)
-            if n == 3:
-                h_quantise(0)
-            if n == 5:
-                h_quantise(1)
-            if n == 9:
+            if n == 10:
                 o1_sb = keep.tile([P, P], F32)
                 nc.vector.tensor_copy(out=o1_sb[:], in_=banks["o1"][:, 0:P])
                 nc.sync.dma_start(out=o1.rearrange("(i p) o -> i (p o)", p=P), in_=o1_sb[0:NT, :])

@@ -209,45 +209,32 @@ def tile_adaptiveinputsoftmax_pa_kernel(tc, x, head_weight, tail_proj_0, tail_w_
 
         small = {}
 
-        def bank_max(n, chunks):
-            if ("m4", n) not in small:
-                m4 = stats.tile([P, 4], F32, name="m4")
-                small[("m4", n)] = m4
-            for c in chunks:
-                nc.vector.tensor_reduce(
-                    out=small[("m4", n)][:, c : c + 1], in_=banks[(n, c)][:], axis=AX.X, op=ALU.max
+        def row_max(n):
+            e = big.tile([P, V], F32, tag="big", name="e")
+            small[("e", n)] = e
+            m4 = stats.tile([P, 4], F32, name="m4")
+            for c in range(4):
+                nc.vector.tensor_scalar(
+                    out=e[:, BANK * c : BANK * c + BANK], in0=banks[(n, c)][:], scalar1=1.0, scalar2=None,
+                    op0=ALU.mult, op1=ALU.max, accum_out=m4[:, c : c + 1],
                 )
-
-        def set_max(n):
             negm = stats.tile([P, 1], F32, name="negm")
-            nc.vector.tensor_reduce(out=negm[:], in_=small[("m4", n)][:], axis=AX.X, op=ALU.max, negate=True)
+            nc.vector.tensor_reduce(out=negm[:], in_=m4[:], axis=AX.X, op=ALU.max, negate=True)
             small[("negm", n)] = negm
 
-        def row_max(n):
-            bank_max(n, (0, 1, 2, 3))
-            set_max(n)
-
         def exps(n):
-            e = big.tile([P, V], F32, tag="big", name="e")
-            s4 = stats.tile([P, 4], F32, name="s4")
-            small[("e", n)] = e
-            small[("s4", n)] = s4
-            for c in range(4):
-                nc.scalar.activation(
-                    out=e[:, BANK * c : BANK * c + BANK],
-                    in_=banks[(n, c)][:],
-                    func=ACT.Exp,
-                    bias=small[("negm", n)][:, 0:1],
-                    scale=1.0,
-                    accum_out=s4[:, c : c + 1],
-                )
+            e = small[("e", n)]
+            s = stats.tile([P, 1], F32, name="s")
+            small[("s", n)] = s
+            nc.scalar.activation(
+                out=e[:], in_=e[:], func=ACT.Exp, bias=small[("negm", n)][:, 0:1], scale=1.0, accum_out=s[:]
+            )
 
         def finish(n):
             i = n % NT
             rows = slice(P * i, P * i + P)
             e = small[("e", n)]
-            s = stats.tile([P, 1], F32, name="s")
-            nc.vector.tensor_reduce(out=s[:], in_=small[("s4", n)][:], axis=AX.X, op=ALU.add)
+            s = small[("s", n)]
             r = stats.tile([P, 1], F32, name="r")
             nc.vector.reciprocal(out=r[:], in_=s[:])
             if n < NT:
@@ -305,42 +292,37 @@ def tile_adaptiveinputsoftmax_pa_kernel(tc, x, head_weight, tail_proj_0, tail_w_
         for i in range(NT):
             x_quantise(i)
         logits(0)
+        logits(1)
         regroup("C1", True)
         regroup("C0", False)
-        for i in range(4):
-            h_matmuls(i)
-        bank_max(0, (0, 1))
+        row_max(0)
         quantise("C0")
+        regroup("C2", True)
         regroup("C3", True)
-        regroup("C2", False)
         quantise("C1")
-        for i in range(4):
-            h_out(i)
-        bank_max(0, (2, 3))
-        set_max(0)
-        quantise("C2")
-        quantise("C3")
-        for i in range(4, NT):
-            h_matmuls(i)
-        for i in range(4, NT):
-            h_out(i)
-        h_quantise(0)
-        logits(1)
-        bank_max(1, (0, 1))
-        h_quantise(1)
-        bank_max(1, (2, 3))
-        set_max(1)
 
+        h_tiles = {1: (0, 1), 2: (2, 3), 3: (4, 5), 4: (6, 7)}
         for n in range(2 * NT):
-            if 1 <= n < 2 * NT - 1:
-                logits(n + 1)
+            if n + 2 < 2 * NT:
+                logits(n + 2)
             exps(n)
-            if n == 10:
+            if n + 1 < 2 * NT:
+                row_max(n + 1)
+            if n == 0:
+                quantise("C2")
+                quantise("C3")
+            for i in h_tiles.get(n, ()):
+                h_matmuls(i)
+            for i in h_tiles.get(n, ()):
+                h_out(i)
+            if n == 9:
                 o1_bank = new_bank("o1")
                 nc.tensor.transpose(o1_bank[:, 0:P], cl[:, 1, :], ident[:])
-            if 1 <= n < 2 * NT - 1:
-                row_max(n + 1)
-            if n == 10:
+            if n == 4:
+                h_quantise(0)
+            if n == 5:
+                h_quantise(1)
+            if n == 9:
                 o1_sb = keep.tile([P, P], F32)
                 nc.vector.tensor_copy(out=o1_sb[:], in_=banks["o1"][:, 0:P])
                 nc.sync.dma_start(out=o1.rearrange("(i p) o -> i (p o)", p=P), in_=o1_sb[0:NT, :])

@@ -234,14 +234,10 @@ def tile_adaptiveinputsoftmax_pa_kernel(tc, x, head_weight, tail_proj_0, tail_w_
             i = n % NT
             rows = slice(P * i, P * i + P)
             e = small[("e", n)]
-            s = small[("s", n)]
             r = stats.tile([P, 1], F32, name="r")
-            nc.vector.reciprocal(out=r[:], in_=s[:])
+            small[("r", n)] = r
+            nc.vector.reciprocal(out=r[:], in_=small[("s", n)][:])
             if n < NT:
-                nc.gpsimd.tensor_scalar(
-                    out=cl[:, :, i], in0=e[:, HEAD_TOKENS:V], scalar1=r[:, 0:1], scalar2=0.0,
-                    op0=ALU.mult, op1=ALU.add,
-                )
                 nc.gpsimd.tensor_scalar(
                     out=e[:, 0:HEAD_TOKENS], in0=e[:, 0:HEAD_TOKENS],
                     scalar1=r[:, 0:1], scalar2=0.0, op0=ALU.mult, op1=ALU.add,
@@ -256,7 +252,7 @@ def tile_adaptiveinputsoftmax_pa_kernel(tc, x, head_weight, tail_proj_0, tail_w_
             elif n == 2 * NT - 2:
                 for hf in range(2):
                     cols = slice(1024 * hf, 1024 * hf + 1024)
-                    nc.gpsimd.tensor_scalar(
+                    nc.vector.tensor_scalar(
                         out=e[:, cols], in0=e[:, cols],
                         scalar1=r[:, 0:1], scalar2=cl[:, 0, i : i + 1], op0=ALU.mult, op1=ALU.mult,
                     )
@@ -276,6 +272,11 @@ def tile_adaptiveinputsoftmax_pa_kernel(tc, x, head_weight, tail_proj_0, tail_w_
                 )
                 nc.sync.dma_start(out=o0[rows, HEAD_TOKENS : HEAD_TOKENS + LAST_SPLIT], in_=e[:, 0:LAST_SPLIT])
                 nc.sync.dma_start(out=o0[rows, HEAD_TOKENS + LAST_SPLIT : HEAD_TOKENS + V], in_=e[:, LAST_SPLIT:V])
+
+        def cluster_columns(n):
+            nc.scalar.activation(
+                out=cl[:, :, n], in_=small[("e", n)][:, HEAD_TOKENS:V], func=ACT.Copy, scale=small[("r", n)][:, 0:1]
+            )
 
         first = ["A0", "A1", "B0", "B1", "B2", "B3", "B4", "B5", "B6", "B7"]
         for k in range(5):
@@ -306,6 +307,8 @@ def tile_adaptiveinputsoftmax_pa_kernel(tc, x, head_weight, tail_proj_0, tail_w_
             if n + 2 < 2 * NT:
                 logits(n + 2)
             exps(n)
+            if 1 <= n <= NT:
+                cluster_columns(n - 1)
             if n + 1 < 2 * NT:
                 row_max(n + 1)
             if n == 0:

@@ -234,15 +234,21 @@ def tile_adaptiveinputsoftmax_pa_kernel(tc, x, head_weight, tail_proj_0, tail_w_
             i = n % NT
             rows = slice(P * i, P * i + P)
             e = small[("e", n)]
+            s = small[("s", n)]
             r = stats.tile([P, 1], F32, name="r")
-            small[("r", n)] = r
-            nc.vector.reciprocal(out=r[:], in_=small[("s", n)][:])
+            nc.vector.reciprocal(out=r[:], in_=s[:])
             if n < NT:
+                cuts = (0, 1024, HEAD_TOKENS) if n == 0 else (0, HEAD_TOKENS)
+                for lo, hi in zip(cuts[:-1], cuts[1:]):
+                    nc.gpsimd.tensor_scalar(
+                        out=e[:, lo:hi], in0=e[:, lo:hi],
+                        scalar1=r[:, 0:1], scalar2=0.0, op0=ALU.mult, op1=ALU.add,
+                    )
+                    nc.sync.dma_start(out=o0[rows, lo:hi], in_=e[:, lo:hi])
                 nc.gpsimd.tensor_scalar(
-                    out=e[:, 0:HEAD_TOKENS], in0=e[:, 0:HEAD_TOKENS],
-                    scalar1=r[:, 0:1], scalar2=0.0, op0=ALU.mult, op1=ALU.add,
+                    out=cl[:, :, i], in0=e[:, HEAD_TOKENS:V], scalar1=r[:, 0:1], scalar2=0.0,
+                    op0=ALU.mult, op1=ALU.add,
                 )
-                nc.sync.dma_start(out=o0[rows, 0:HEAD_TOKENS], in_=e[:, 0:HEAD_TOKENS])
             elif n < 2 * NT - 2:
                 nc.gpsimd.tensor_scalar(
                     out=e[:], in0=e[:],
@@ -252,7 +258,7 @@ def tile_adaptiveinputsoftmax_pa_kernel(tc, x, head_weight, tail_proj_0, tail_w_
             elif n == 2 * NT - 2:
                 for hf in range(2):
                     cols = slice(1024 * hf, 1024 * hf + 1024)
-                    nc.vector.tensor_scalar(
+                    nc.gpsimd.tensor_scalar(
                         out=e[:, cols], in0=e[:, cols],
                         scalar1=r[:, 0:1], scalar2=cl[:, 0, i : i + 1], op0=ALU.mult, op1=ALU.mult,
                     )
@@ -273,11 +279,6 @@ def tile_adaptiveinputsoftmax_pa_kernel(tc, x, head_weight, tail_proj_0, tail_w_
                 nc.sync.dma_start(out=o0[rows, HEAD_TOKENS : HEAD_TOKENS + LAST_SPLIT], in_=e[:, 0:LAST_SPLIT])
                 nc.sync.dma_start(out=o0[rows, HEAD_TOKENS + LAST_SPLIT : HEAD_TOKENS + V], in_=e[:, LAST_SPLIT:V])
 
-        def cluster_columns(n):
-            nc.scalar.activation(
-                out=cl[:, :, n], in_=small[("e", n)][:, HEAD_TOKENS:V], func=ACT.Copy, scale=small[("r", n)][:, 0:1]
-            )
-
         first = ["A0", "A1", "B0", "B1", "B2", "B3", "B4", "B5", "B6", "B7"]
         for k in range(5):
             regroup(first[2 * k + 1], True)
@@ -295,25 +296,25 @@ def tile_adaptiveinputsoftmax_pa_kernel(tc, x, head_weight, tail_proj_0, tail_w_
         logits(0)
         logits(1)
         regroup("C1", True)
-        regroup("C0", False)
         row_max(0)
-        quantise("C0")
-        regroup("C2", True)
-        regroup("C3", True)
+        regroup("C0", False)
         quantise("C1")
+        quantise("C0")
 
-        h_tiles = {1: (0, 1), 2: (2, 3), 3: (4, 5), 4: (6, 7)}
+        h_tiles = {1: (0, 1), 2: (2, 3), 5: (4, 5), 6: (6, 7)}
+        late_units = {0: "C2", 3: "C3"}
         for n in range(2 * NT):
             if n + 2 < 2 * NT:
                 logits(n + 2)
             exps(n)
-            if 1 <= n <= NT:
-                cluster_columns(n - 1)
+            if n in late_units:
+                regroup(late_units[n], True)
+            if n == 0:
+                finish(n)
             if n + 1 < 2 * NT:
                 row_max(n + 1)
-            if n == 0:
-                quantise("C2")
-                quantise("C3")
+            if n - 1 in late_units:
+                quantise(late_units[n - 1])
             for i in h_tiles.get(n, ()):
                 h_matmuls(i)
             for i in h_tiles.get(n, ()):
@@ -321,12 +322,13 @@ def tile_adaptiveinputsoftmax_pa_kernel(tc, x, head_weight, tail_proj_0, tail_w_
             if n == 9:
                 o1_bank = new_bank("o1")
                 nc.tensor.transpose(o1_bank[:, 0:P], cl[:, 1, :], ident[:])
-            if n == 4:
+            if n == 3:
                 h_quantise(0)
-            if n == 5:
+            if n == 7:
                 h_quantise(1)
             if n == 9:
                 o1_sb = keep.tile([P, P], F32)
                 nc.vector.tensor_copy(out=o1_sb[:], in_=banks["o1"][:, 0:P])
                 nc.sync.dma_start(out=o1.rearrange("(i p) o -> i (p o)", p=P), in_=o1_sb[0:NT, :])
-            finish(n)
+            if n > 0:
+                finish(n)

from contextlib import ExitStack

import concourse.mybir as mybir
from concourse.masks import make_identity

F32 = mybir.dt.float32
BF16 = mybir.dt.bfloat16
U32 = mybir.dt.uint32
U8 = mybir.dt.uint8
FP8X4 = mybir.dt.float8_e4m3fn_x4
ALU = mybir.AluOpType
ACT = mybir.ActivationFunctionType
AX = mybir.AxisListType

P = 128
TOKENS = 1024
D = 1024
V = 2048
P0 = 512
NT = TOKENS // P
HEAD_TOKENS = 2046
BANK = 512
LAST_SPLIT = 1344
BIG_BUFS = 13

FLOPS = 2 * TOKENS * (D * V + D * P0 + P0 * V)


def tile_adaptiveinputsoftmax_pa_kernel(tc, x, head_weight, tail_proj_0, tail_w_0, out_0, out_1):
    nc = tc.nc
    xf = x.flatten_outer_dims()
    o0 = out_0.flatten_outer_dims()
    o1 = out_1.flatten_outer_dims()

    with ExitStack() as ctx:
        ctx.enter_context(tc.manual_schedule())
        keep = ctx.enter_context(tc.tile_pool(name="keep", bufs=1))
        gwp = ctx.enter_context(tc.tile_pool(name="gwp", bufs=5))
        big = ctx.enter_context(tc.tile_pool(name="big", bufs=BIG_BUFS))
        stats = ctx.enter_context(tc.tile_pool(name="stats", bufs=4))
        psum = ctx.enter_context(tc.psum_pool(name="psum", bufs=8))

        tp_raw = big.tile([P, 2, 4, P0], BF16, tag="big", name="tp_raw")
        for g in range(2):
            nc.sync.dma_start(
                out=tp_raw[:, g, :, :].rearrange("p (u e) c -> p u (e c)", u=2),
                in_=tail_proj_0[512 * g : 512 * g + 512, :].rearrange("(u q e) c -> q u (e c)", u=2, e=2),
            )
        hw_raw = {}
        for g in range(2):
            for hf in range(2):
                hw_part = big.tile([P, 4, 1024], BF16, tag="big", name="hw_part")
                hw_raw[(g, hf)] = hw_part
                for u in range(2):
                    r0 = 512 * g + 256 * u
                    nc.sync.dma_start(
                        out=hw_part[:, 2 * u : 2 * u + 2, :],
                        in_=head_weight[r0 : r0 + 256, 1024 * hf : 1024 * hf + 1024].rearrange(
                            "(q e) c -> q e c", e=2
                        ),
                    )
        x_raw = {}
        for b in range(2):
            x_part = big.tile([P, 4, D], BF16, tag="big", name="x_part")
            x_raw[b] = x_part
            for a in range(2):
                t0 = 512 * b + 256 * a
                nc.sync.dma_start(
                    out=x_part[:, 2 * a : 2 * a + 2, :],
                    in_=xf[t0 : t0 + 256, :].rearrange("(i p) k -> p i k", p=P),
                )
        tw_raw = {}
        for hf in range(2):
            tw_part = big.tile([P, 4, 1024], BF16, tag="big", name="tw_part")
            tw_raw[hf] = tw_part
            nc.sync.dma_start(
                out=tw_part[:],
                in_=tail_w_0[:, 1024 * hf : 1024 * hf + 1024].rearrange("(t p) n -> p t n", p=P),
            )

        warm_in = keep.tile([P, 1], F32)
        warm_out = keep.tile([P, 1], F32)
        nc.vector.memset(warm_in[:], 0.0)
        nc.scalar.activation(out=warm_out[:], in_=warm_in[:], func=ACT.Exp)
        cl = keep.tile([P, 2, P], F32)
        nc.vector.memset(cl[:], 0.0)
        ident = keep.tile([P, P], F32)
        make_identity(nc, ident[:])

        x_codes = keep.tile([P, NT, 2 * P], U32, align_bytes=64)
        x_scales = keep.tile([P, NT, 2 * P], U8, align_bytes=64)
        tp_codes = keep.tile([P, 2, P0], U32, align_bytes=64)
        tp_scales = keep.tile([P, 2, P0], U8, align_bytes=64)
        hw_codes = keep.tile([P, 2, V], U32, align_bytes=64)
        hw_scales = keep.tile([P, 2, V], U8, align_bytes=64)
        tw_codes = keep.tile([P, V], U32, align_bytes=64)
        tw_scales = keep.tile([P, V], U8, align_bytes=64)
        gx = keep.tile([P, NT, 2, P, 2], F32, align_bytes=64)
        gh = keep.tile([P, NT, P, 4], BF16, align_bytes=64)
        h_codes = keep.tile([P, NT * P], U32, align_bytes=64)
        h_scales = keep.tile([P, NT * P], U8, align_bytes=64)

        units = {}
        for g in range(2):
            units["A%d" % g] = (tp_raw[:, g, :, :], tp_codes[:, g, :], tp_scales[:, g, :])
        for n in range(8):
            g, c = divmod(n, 4)
            cols = slice(BANK * c, BANK * c + BANK)
            part = slice(BANK * (c % 2), BANK * (c % 2) + BANK)
            units["B%d" % n] = (hw_raw[(g, c // 2)][:, :, part], hw_codes[:, g, cols], hw_scales[:, g, cols])
        for c in range(4):
            cols = slice(BANK * c, BANK * c + BANK)
            part = slice(BANK * (c % 2), BANK * (c % 2) + BANK)
            units["C%d" % c] = (tw_raw[c // 2][:, :, part], tw_codes[:, cols], tw_scales[:, cols])
        grouped = {}

        def regroup(u, on_scalar):
            gw = gwp.tile([P, BANK, 4], BF16, align_bytes=64, name="gw")
            grouped[u] = gw
            dst_v = gw[:].rearrange("p (c i) t -> p c t i", i=4)
            src_v = units[u][0].rearrange("p t (c i) -> p c t i", i=4)
            if on_scalar:
                nc.scalar.copy(out=dst_v, in_=src_v)
            else:
                nc.vector.tensor_copy(out=dst_v, in_=src_v)

        def quantise(u):
            nc.vector.quantize_mx(
                out=units[u][1].bitcast(FP8X4),
                scales=units[u][2],
                in_=grouped[u][:].rearrange("p w t -> p (w t)"),
            )

        banks = {}

        def new_bank(key):
            bank = psum.tile([P, BANK], F32, tag="bank", name="bank")
            banks[key] = bank
            return bank

        def x_transpose(i):
            xw = x_raw[i // 4][:, i % 4, :].bitcast(F32)
            bank = new_bank(("x", i))
            for c in range(4):
                nc.tensor.transpose(bank[:, P * c : P * c + P], xw[:, P * c : P * c + P], ident[:])

        def x_out(i):
            nc.scalar.copy(
                out=gx[:, i, :, :, :], in_=banks[("x", i)][:].rearrange("p (g u r) -> p g r u", g=2, u=2)
            )

        def x_quantise(i):
            nc.vector.quantize_mx(
                out=x_codes[:, i, :].bitcast(FP8X4),
                scales=x_scales[:, i, :],
                in_=gx[:, i, :, :, :].rearrange("p g r u -> p (g r u)").bitcast(BF16),
            )

        def h_matmuls(i):
            bank = new_bank(("h", i))
            for j in range(4):
                for g in range(2):
                    nc.tensor.matmul_mx(
                        out=bank[:, P * j : P * j + P],
                        lhsT=tp_codes[:, g, P * j : P * j + P].bitcast(FP8X4),
                        lhsT_scale=tp_scales[:, g, P * j : P * j + P],
                        rhs=x_codes[:, i, P * g : P * g + P].bitcast(FP8X4),
                        rhs_scale=x_scales[:, i, P * g : P * g + P],
                        start=(g == 0),
                        stop=(g == 1),
                    )

        def h_out(i):
            nc.scalar.copy(out=gh[:, i, :, :], in_=banks[("h", i)][:].rearrange("p (j r) -> p r j", j=4))

        def h_quantise(a):
            nc.vector.quantize_mx(
                out=h_codes[:, 512 * a : 512 * a + 512].bitcast(FP8X4),
                scales=h_scales[:, 512 * a : 512 * a + 512],
                in_=gh[:, 4 * a : 4 * a + 4, :, :].rearrange("p i r j -> p (i r j)"),
            )

        def logits(n):
            i = n % NT
            for c in range(4):
                cols = slice(BANK * c, BANK * c + BANK)
                bank = new_bank((n, c))
                if n < NT:
                    for g in range(2):
                        nc.tensor.matmul_mx(
                            out=bank[:],
                            lhsT=x_codes[:, i, P * g : P * g + P].bitcast(FP8X4),
                            lhsT_scale=x_scales[:, i, P * g : P * g + P],
                            rhs=hw_codes[:, g, cols].bitcast(FP8X4),
                            rhs_scale=hw_scales[:, g, cols],
                            start=(g == 0),
                            stop=(g == 1),
                        )
                else:
                    nc.tensor.matmul_mx(
                        out=bank[:],
                        lhsT=h_codes[:, P * i : P * i + P].bitcast(FP8X4),
                        lhsT_scale=h_scales[:, P * i : P * i + P],
                        rhs=tw_codes[:, cols].bitcast(FP8X4),
                        rhs_scale=tw_scales[:, cols],
                        start=True,
                        stop=True,
                    )

        small = {}

        def row_max(n):
            e = big.tile([P, V], F32, tag="big", name="e")
            small[("e", n)] = e
            m4 = stats.tile([P, 4], F32, name="m4")
            for c in range(4):
                nc.vector.tensor_scalar(
                    out=e[:, BANK * c : BANK * c + BANK], in0=banks[(n, c)][:], scalar1=1.0, scalar2=None,
                    op0=ALU.mult, op1=ALU.max, accum_out=m4[:, c : c + 1],
                )
            negm = stats.tile([P, 1], F32, name="negm")
            nc.vector.tensor_reduce(out=negm[:], in_=m4[:], axis=AX.X, op=ALU.max, negate=True)
            small[("negm", n)] = negm

        def exps(n):
            e = small[("e", n)]
            s = stats.tile([P, 1], F32, name="s")
            small[("s", n)] = s
            nc.scalar.activation(
                out=e[:], in_=e[:], func=ACT.Exp, bias=small[("negm", n)][:, 0:1], scale=1.0, accum_out=s[:]
            )

        def finish(n):
            i = n % NT
            rows = slice(P * i, P * i + P)
            e = small[("e", n)]
            s = small[("s", n)]
            r = stats.tile([P, 1], F32, name="r")
            nc.vector.reciprocal(out=r[:], in_=s[:])
            if n < NT:
                cuts = (0, 1024, HEAD_TOKENS) if n == 0 else (0, HEAD_TOKENS)
                for lo, hi in zip(cuts[:-1], cuts[1:]):
                    nc.gpsimd.tensor_scalar(
                        out=e[:, lo:hi], in0=e[:, lo:hi],
                        scalar1=r[:, 0:1], scalar2=0.0, op0=ALU.mult, op1=ALU.add,
                    )
                    nc.sync.dma_start(out=o0[rows, lo:hi], in_=e[:, lo:hi])
                nc.gpsimd.tensor_scalar(
                    out=cl[:, :, i], in0=e[:, HEAD_TOKENS:V], scalar1=r[:, 0:1], scalar2=0.0,
                    op0=ALU.mult, op1=ALU.add,
                )
            elif n < 2 * NT - 2:
                nc.gpsimd.tensor_scalar(
                    out=e[:], in0=e[:],
                    scalar1=r[:, 0:1], scalar2=cl[:, 0, i : i + 1], op0=ALU.mult, op1=ALU.mult,
                )
                nc.sync.dma_start(out=o0[rows, HEAD_TOKENS : HEAD_TOKENS + V], in_=e[:])
            elif n == 2 * NT - 2:
                for hf in range(2):
                    cols = slice(1024 * hf, 1024 * hf + 1024)
                    nc.gpsimd.tensor_scalar(
                        out=e[:, cols], in0=e[:, cols],
                        scalar1=r[:, 0:1], scalar2=cl[:, 0, i : i + 1], op0=ALU.mult, op1=ALU.mult,
                    )
                    nc.sync.dma_start(
                        out=o0[rows, HEAD_TOKENS + 1024 * hf : HEAD_TOKENS + 1024 * hf + 1024], in_=e[:, cols]
                    )
            else:
                rc = stats.tile([P, 1], F32, name="rc")
                nc.vector.tensor_scalar(
                    out=rc[:], in0=r[:], scalar1=cl[:, 0, i : i + 1], scalar2=None, op0=ALU.mult
                )
                nc.vector.tensor_scalar(
                    out=e[:, 0:LAST_SPLIT], in0=e[:, 0:LAST_SPLIT], scalar1=rc[:, 0:1], scalar2=None, op0=ALU.mult
                )
                nc.scalar.activation(
                    out=e[:, LAST_SPLIT:V], in_=e[:, LAST_SPLIT:V], func=ACT.Copy, scale=rc[:, 0:1]
                )
                nc.sync.dma_start(out=o0[rows, HEAD_TOKENS : HEAD_TOKENS + LAST_SPLIT], in_=e[:, 0:LAST_SPLIT])
                nc.sync.dma_start(out=o0[rows, HEAD_TOKENS + LAST_SPLIT : HEAD_TOKENS + V], in_=e[:, LAST_SPLIT:V])

        first = ["A0", "A1", "B0", "B1", "B2", "B3", "B4", "B5", "B6", "B7"]
        for k in range(5):
            regroup(first[2 * k + 1], True)
            regroup(first[2 * k], False)
            if k > 0:
                quantise(first[2 * k - 1])
            quantise(first[2 * k])
        for i in range(NT):
            x_transpose(i)
        for i in range(NT):
            x_out(i)
        quantise("B7")
        for i in range(NT):
            x_quantise(i)
        logits(0)
        logits(1)
        regroup("C1", True)
        row_max(0)
        regroup("C0", False)
        quantise("C1")
        quantise("C0")

        h_tiles = {1: (0, 1), 2: (2, 3), 5: (4, 5), 6: (6, 7)}
        late_units = {0: "C2", 3: "C3"}
        for n in range(2 * NT):
            if n + 2 < 2 * NT:
                logits(n + 2)
            exps(n)
            if n in late_units:
                regroup(late_units[n], True)
            if n == 0:
                finish(n)
            if n + 1 < 2 * NT:
                row_max(n + 1)
            if n - 1 in late_units:
                quantise(late_units[n - 1])
            for i in h_tiles.get(n, ()):
                h_matmuls(i)
            for i in h_tiles.get(n, ()):
                h_out(i)
            if n == 9:
                o1_bank = new_bank("o1")
                nc.tensor.transpose(o1_bank[:, 0:P], cl[:, 1, :], ident[:])
            if n == 3:
                h_quantise(0)
            if n == 7:
                h_quantise(1)
            if n == 9:
                o1_sb = keep.tile([P, P], F32)
                nc.vector.tensor_copy(out=o1_sb[:], in_=banks["o1"][:, 0:P])
                nc.sync.dma_start(out=o1.rearrange("(i p) o -> i (p o)", p=P), in_=o1_sb[0:NT, :])
            if n > 0:
                finish(n)
